import numpy as np
import ml_dtypes


def mxq(x, axis, fmt="e4m3"):
    dtype, down = {"e4m3": (ml_dtypes.float8_e4m3fn, 7), "e5m2": (ml_dtypes.float8_e5m2, 14)}[fmt]
    v = np.moveaxis(np.asarray(x, np.float32).astype(ml_dtypes.bfloat16).astype(np.float64), axis, -1)
    blocks = v.reshape(v.shape[:-1] + (-1, 32))
    amax = np.abs(blocks).max(-1, keepdims=True)
    byte = np.maximum(np.where(amax > 0, np.frexp(amax)[1] - 1 + 127, 0) - down, 1)
    scale = np.exp2(byte - 127.0)
    codes = (blocks / scale).astype(np.float32).astype(dtype).astype(np.float64)
    return np.moveaxis((codes * scale).reshape(v.shape), -1, axis)


WIDE = False


def mx_kscale(k):
    if not WIDE:
        return np.ones(k)
    levels = np.array([10, -10, 5, -5, 0])
    if k % 512:
        return np.exp2(np.random.permutation(np.resize(levels, k // 32))).repeat(32)
    a = np.empty((k // 512, 16))
    for p in range(k // 512):
        a[p, :8] = np.random.permutation(np.resize(levels, 8))
        for g in range(8):
            far = levels[np.abs(levels - a[p, g]) >= 10]
            a[p, g + 8] = far[np.random.randint(len(far))]
    return np.exp2(a.ravel()).repeat(32)


BF16 = ml_dtypes.bfloat16


def bf(x):
    return np.asarray(x, np.float32).astype(BF16)


def f64(x):
    return np.asarray(x).astype(np.float64)


N, MUL, RANK, D0, D1, D2 = 1024, 512, 128, 1, 3, 5
DIMS = (D0, D1, D2)
SD = D0 + D1 + D2
NI = len(DIMS)
SCALING = 2.0


def setup_inputs():
    s = mx_kscale(MUL)
    return {"x": bf(np.random.standard_normal((N, SD * MUL)) * np.tile(s, SD)),
            "a_lora": bf(np.random.standard_normal((N, SD * RANK)) * 0.5),
            "w_base": bf(np.random.standard_normal((NI, MUL, MUL)) / s[None, :, None]),
            "w_lora_b": bf(np.random.standard_normal((NI, RANK, MUL)))}


def reference(x, a_lora, w_base, w_lora_b):
    x, a_lora, w_base, w_lora_b = f64(x), f64(a_lora), f64(w_base), f64(w_lora_b)
    pw_base = 1.0 / np.sqrt(MUL)
    pw_b = 1.0 / np.sqrt(RANK)
    n = x.shape[0]
    outs = []
    off = 0
    offa = 0
    for k, d in enumerate(DIMS):
        seg = x[:, off:off + d * MUL].reshape(n * d, MUL)
        y = pw_base * (mxq(seg, 1, "e4m3") @ mxq(w_base[k], 0, "e4m3"))
        a = a_lora[:, offa:offa + d * RANK].reshape(n * d, RANK)
        b = pw_b * (a @ w_lora_b[k])
        outs.append((y + SCALING * b).reshape(n, d * MUL))
        off += d * MUL
        offa += d * RANK
    return np.concatenate(outs, axis=-1)

@@ -1,0 +1,229 @@
+import math
+from contextlib import ExitStack
+
+import concourse.mybir as mybir
+from concourse.masks import make_identity
+
+F32 = mybir.dt.float32
+BF16 = mybir.dt.bfloat16
+U32 = mybir.dt.uint32
+U8 = mybir.dt.uint8
+FP8X4 = mybir.dt.float8_e4m3fn_x4
+MULT = mybir.AluOpType.mult
+ADD = mybir.AluOpType.add
+
+P = 128
+PACK = 4
+NODES = 1024
+MUL = 512
+RANK = 128
+IRREP_OF_BLOCK = (0, 1, 1, 1, 2, 2, 2, 2, 2)
+BLOCKS = len(IRREP_OF_BLOCK)
+IRREPS = 3
+FIRST_USE = {
+    BLOCKS - 1 - j: IRREP_OF_BLOCK[j]
+    for j in range(BLOCKS)
+    if j == BLOCKS - 1 or IRREP_OF_BLOCK[j + 1] != IRREP_OF_BLOCK[j]
+}
+ROW_TILES = NODES // P
+PAIR = 2
+PAIRS = ROW_TILES // PAIR
+STEPS = PAIRS * BLOCKS
+HALVES = 2
+GROUP = 3
+LOOKAHEAD = 2
+WEIGHT_LEAD = 5
+STAGE_BUFS = 6
+
+BASE_FACTOR = 1.0 / math.sqrt(MUL)
+LORA_FACTOR = 2.0 / math.sqrt(RANK)
+
+FLOPS = 2 * NODES * BLOCKS * MUL * (MUL + RANK)
+
+
+def tile_loracuetlinear_pa_t_kernel(tc, x, a_lora, w_base, w_lora_b, out):
+    nc = tc.nc
+    x_rows = x.rearrange("(p r) c -> p r c", r=ROW_TILES)
+    a_rows = a_lora.rearrange("(p r) c -> p r c", r=ROW_TILES)
+    out_rows = out.rearrange("(p r) c -> p r c", r=ROW_TILES)
+
+    with ExitStack() as ctx:
+        keep = ctx.enter_context(tc.tile_pool(name="keep", bufs=1))
+        w_work = ctx.enter_context(tc.tile_pool(name="w_work", bufs=2))
+        x_work = ctx.enter_context(tc.tile_pool(name="x_work", bufs=3))
+        ready = ctx.enter_context(tc.tile_pool(name="ready", bufs=LOOKAHEAD + 2))
+        a_ready = ctx.enter_context(tc.tile_pool(name="a_ready", bufs=3))
+        stages = ctx.enter_context(tc.tile_pool(name="stages", bufs=STAGE_BUFS))
+        xt_banks = ctx.enter_context(tc.psum_pool(name="xt_banks", bufs=2))
+        at_banks = ctx.enter_context(tc.psum_pool(name="at_banks", bufs=1))
+        lora_banks = ctx.enter_context(tc.psum_pool(name="lora_banks", bufs=2))
+        base_banks = ctx.enter_context(tc.psum_pool(name="base_banks", bufs=3))
+        ctx.enter_context(tc.manual_schedule())
+
+        def pieces(pair):
+            return BLOCKS // GROUP if pair == 0 else 1
+
+        def row_tiles(name, width):
+            return [
+                [
+                    keep.tile([P, PAIR * (BLOCKS // pieces(pair)) * width], BF16, name="%s%d%d" % (name, pair, piece))
+                    for piece in range(pieces(pair))
+                ]
+                for pair in range(PAIRS)
+            ]
+
+        x_sb = row_tiles("x_sb", MUL)
+        a_sb = row_tiles("a_sb", RANK)
+        w_raw = [keep.tile([P, PACK * MUL], BF16, name="w_raw%d" % k) for k in range(IRREPS)]
+        w_codes = [keep.tile([P, MUL], U32, name="w_codes%d" % k, align_bytes=64) for k in range(IRREPS)]
+        w_scales = [keep.tile([P, MUL], U8, name="w_scales%d" % k, align_bytes=64) for k in range(IRREPS)]
+        wb_sb = [keep.tile([P, MUL], BF16, name="wb_sb%d" % k) for k in range(IRREPS)]
+        ident_f32 = keep.tile([P, P], F32, name="ident_f32")
+        ident_bf16 = keep.tile([P, P], BF16, name="ident_bf16")
+
+        def place(step):
+            pair, position = divmod(step, BLOCKS)
+            return pair, BLOCKS - 1 - position
+
+        def load_rows(pair, piece):
+            rows = slice(PAIR * pair, PAIR * (pair + 1))
+            blocks = BLOCKS // pieces(pair)
+            for sb, dram, width in ((x_sb, x_rows, MUL), (a_sb, a_rows, RANK)):
+                cols = slice(piece * blocks * width, (piece + 1) * blocks * width)
+                nc.sync.dma_start(
+                    out=sb[pair][piece][:].rearrange("p (i c) -> p i c", i=PAIR), in_=dram[:, rows, cols]
+                )
+
+        def block_of(sb, pair, i, j, width):
+            blocks = BLOCKS // pieces(pair)
+            return sb[pair][j // blocks], (i * blocks + j % blocks) * width
+
+        def load_weights(k):
+            nc.sync.dma_start(out=w_raw[k][:], in_=w_base[k, :, :].rearrange("(q t) c -> q (t c)", t=PACK))
+            nc.sync.dma_start(out=wb_sb[k][:], in_=w_lora_b[k, :, :])
+
+        def quantise_weights(k):
+            w_grouped = w_work.tile([P, MUL, PACK], BF16, name="w_grouped", align_bytes=64)
+            nc.vector.tensor_copy(
+                out=w_grouped[:].rearrange("q (c r) t -> q c t r", r=4),
+                in_=w_raw[k][:].rearrange("q (t c r) -> q c t r", t=PACK, r=4),
+            )
+            nc.vector.quantize_mx(
+                out=w_codes[k][:].bitcast(FP8X4),
+                scales=w_scales[k][:],
+                in_=w_grouped[:].rearrange("q c t -> q (c t)"),
+            )
+
+        def transpose_row_tile(step, i, xt, at):
+            pair, j = place(step)
+            x_tile, first = block_of(x_sb, pair, i, j, MUL)
+            for u in range(HALVES):
+                words = slice(first // 2 + u, first // 2 + HALVES * P, HALVES)
+                nc.tensor.transpose(xt[:, i, u, :], x_tile[:].bitcast(F32)[:, words], ident_f32[:])
+            if step % GROUP == 0:
+                for later in range(GROUP):
+                    a_tile, first = block_of(a_sb, pair, i, j - later, RANK)
+                    nc.tensor.transpose(at[:, later, i, :], a_tile[:, first : first + RANK], ident_bf16[:])
+
+        load_weights(2)
+        load_rows(0, 2)
+        load_weights(1)
+        load_rows(0, 1)
+        load_weights(0)
+        load_rows(0, 0)
+        for pair in range(1, PAIRS):
+            load_rows(pair, 0)
+
+        make_identity(nc, ident_f32[:])
+        make_identity(nc, ident_bf16[:])
+
+        a_t = {}
+        x_codes = {}
+        x_scales = {}
+        stage = None
+
+        at = None
+        for step in range(-WEIGHT_LEAD, STEPS):
+            ahead = step + LOOKAHEAD
+            multiply = step >= 0
+            prepare = 0 <= ahead < STEPS
+            new_group = prepare and ahead % GROUP == 0
+            if multiply:
+                pair, j = place(step)
+                k = IRREP_OF_BLOCK[j]
+                together = 1 if step >= STEPS - GROUP else GROUP
+                if j % together == together - 1:
+                    stage = stages.tile([P, PAIR, together * MUL], F32, name="stage")
+                cols = slice((j % together) * MUL, (j % together + 1) * MUL)
+            if prepare:
+                xt = xt_banks.tile([P, PAIR, HALVES, P], F32, name="xt")
+            if new_group:
+                at = at_banks.tile([P, GROUP, PAIR, P], BF16, name="at")
+
+            lora = []
+            for i in range(PAIR):
+                if multiply:
+                    lora_ps = lora_banks.tile([P, MUL], F32, name="lora_ps")
+                    nc.tensor.matmul(
+                        lora_ps[:],
+                        lhsT=a_t[step // GROUP][:, step % GROUP, i, :],
+                        rhs=wb_sb[k][:],
+                        start=True,
+                        stop=True,
+                    )
+                    lora.append(lora_ps)
+                if prepare:
+                    transpose_row_tile(ahead, i, xt, at)
+
+            if multiply:
+                for i in range(PAIR):
+                    nc.scalar.mul(out=stage[:, i, cols], in_=lora[i][:], mul=LORA_FACTOR)
+            if prepare:
+                x_grouped = x_work.tile([P, PAIR * P * PACK], BF16, name="x_grouped", align_bytes=64)
+                nc.scalar.copy(
+                    out=x_grouped[:].bitcast(F32).rearrange("q (i n u) -> q i n u", i=PAIR, u=HALVES),
+                    in_=xt[:].rearrange("q i u n -> q i n u"),
+                )
+
+            base = []
+            if multiply:
+                for i in range(PAIR):
+                    nodes = slice(i * P, (i + 1) * P)
+                    base_ps = base_banks.tile([P, MUL], F32, name="base_ps")
+                    nc.tensor.matmul_mx(
+                        out=base_ps[:],
+                        lhsT=x_codes[step][:, nodes].bitcast(FP8X4),
+                        lhsT_scale=x_scales[step][:, nodes],
+                        rhs=w_codes[k][:].bitcast(FP8X4),
+                        rhs_scale=w_scales[k][:],
+                        start=True,
+                        stop=True,
+                    )
+                    base.append(base_ps)
+
+            def finish(i):
+                nc.vector.scalar_tensor_tensor(
+                    out=stage[:, i, cols], in0=base[i][:], scalar=BASE_FACTOR, in1=stage[:, i, cols],
+                    op0=MULT, op1=ADD,
+                )
+
+            if step + WEIGHT_LEAD in FIRST_USE:
+                quantise_weights(FIRST_USE[step + WEIGHT_LEAD])
+            if multiply:
+                finish(0)
+            if new_group:
+                a_t[ahead // GROUP] = a_ready.tile([P, GROUP, PAIR, P], BF16, name="a_t")
+                nc.vector.tensor_copy(out=a_t[ahead // GROUP][:], in_=at[:])
+            if multiply:
+                finish(1)
+            if prepare:
+                x_codes[ahead] = ready.tile([P, PAIR * P], U32, name="x_codes", align_bytes=64)
+                x_scales[ahead] = ready.tile([P, PAIR * P], U8, name="x_scales", align_bytes=64)
+                nc.vector.quantize_mx(
+                    out=x_codes[ahead][:].bitcast(FP8X4), scales=x_scales[ahead][:], in_=x_grouped[:]
+                )
+
+            if multiply and j % together == 0:
+                nc.sync.dma_start(
+                    out=out_rows[:, PAIR * pair : PAIR * (pair + 1), j * MUL : (j + together) * MUL], in_=stage[:]
+                )

@@ -21,7 +21,7 @@ IRREP_OF_BLOCK = (0, 1, 1, 1, 2, 2, 2, 2, 2)
 BLOCKS = len(IRREP_OF_BLOCK)
 IRREPS = 3
 FIRST_USE = {
-    BLOCKS - 1 - j: IRREP_OF_BLOCK[j]
+    IRREP_OF_BLOCK[j]: BLOCKS - 1 - j
     for j in range(BLOCKS)
     if j == BLOCKS - 1 or IRREP_OF_BLOCK[j + 1] != IRREP_OF_BLOCK[j]
 }
@@ -31,9 +31,13 @@ PAIRS = ROW_TILES // PAIR
 STEPS = PAIRS * BLOCKS
 HALVES = 2
 GROUP = 3
-LOOKAHEAD = 2
-WEIGHT_LEAD = 5
-STAGE_BUFS = 6
+X_LEAD = 2
+LORA_LEAD = 3
+A_LEAD = 5
+WEIGHT_LEAD = 2
+STAGE_BUFS = 7
+X_PIECES = ((1, 2, 3, 3), (3, 6), (9,), (9,))
+A_PIECES = ((3, 6), (9,), (9,), (9,))
 
 BASE_FACTOR = 1.0 / math.sqrt(MUL)
 LORA_FACTOR = 2.0 / math.sqrt(RANK)
@@ -49,10 +53,9 @@ def tile_loracuetlinear_pa_t_kernel(tc, x, a_lora, w_base, w_lora_b, out):
 
     with ExitStack() as ctx:
         keep = ctx.enter_context(tc.tile_pool(name="keep", bufs=1))
-        w_work = ctx.enter_context(tc.tile_pool(name="w_work", bufs=2))
         x_work = ctx.enter_context(tc.tile_pool(name="x_work", bufs=3))
-        ready = ctx.enter_context(tc.tile_pool(name="ready", bufs=LOOKAHEAD + 2))
-        a_ready = ctx.enter_context(tc.tile_pool(name="a_ready", bufs=3))
+        ready = ctx.enter_context(tc.tile_pool(name="ready", bufs=X_LEAD + 2))
+        a_ready = ctx.enter_context(tc.tile_pool(name="a_ready", bufs=4))
         stages = ctx.enter_context(tc.tile_pool(name="stages", bufs=STAGE_BUFS))
         xt_banks = ctx.enter_context(tc.psum_pool(name="xt_banks", bufs=2))
         at_banks = ctx.enter_context(tc.psum_pool(name="at_banks", bufs=1))
@@ -60,21 +63,19 @@ def tile_loracuetlinear_pa_t_kernel(tc, x, a_lora, w_base, w_lora_b, out):
         base_banks = ctx.enter_context(tc.psum_pool(name="base_banks", bufs=3))
         ctx.enter_context(tc.manual_schedule())
 
-        def pieces(pair):
-            return BLOCKS // GROUP if pair == 0 else 1
+        def cut(pieces, name, width):
+            top = BLOCKS
+            tiles = []
+            for blocks in pieces:
+                top -= blocks
+                tile = keep.tile([P, PAIR * blocks * width], BF16, name="%s_%d" % (name, top))
+                tiles.append((top, blocks, tile))
+            return tiles
 
-        def row_tiles(name, width):
-            return [
-                [
-                    keep.tile([P, PAIR * (BLOCKS // pieces(pair)) * width], BF16, name="%s%d%d" % (name, pair, piece))
-                    for piece in range(pieces(pair))
-                ]
-                for pair in range(PAIRS)
-            ]
-
-        x_sb = row_tiles("x_sb", MUL)
-        a_sb = row_tiles("a_sb", RANK)
+        x_sb = [cut(X_PIECES[pair], "x%d" % pair, MUL) for pair in range(PAIRS)]
+        a_sb = [cut(A_PIECES[pair], "a%d" % pair, RANK) for pair in range(PAIRS)]
         w_raw = [keep.tile([P, PACK * MUL], BF16, name="w_raw%d" % k) for k in range(IRREPS)]
+        w_grouped = [keep.tile([P, MUL, PACK], BF16, name="w_grouped%d" % k, align_bytes=64) for k in range(IRREPS)]
         w_codes = [keep.tile([P, MUL], U32, name="w_codes%d" % k, align_bytes=64) for k in range(IRREPS)]
         w_scales = [keep.tile([P, MUL], U8, name="w_scales%d" % k, align_bytes=64) for k in range(IRREPS)]
         wb_sb = [keep.tile([P, MUL], BF16, name="wb_sb%d" % k) for k in range(IRREPS)]
@@ -85,109 +86,115 @@ def tile_loracuetlinear_pa_t_kernel(tc, x, a_lora, w_base, w_lora_b, out):
             pair, position = divmod(step, BLOCKS)
             return pair, BLOCKS - 1 - position
 
-        def load_rows(pair, piece):
-            rows = slice(PAIR * pair, PAIR * (pair + 1))
-            blocks = BLOCKS // pieces(pair)
-            for sb, dram, width in ((x_sb, x_rows, MUL), (a_sb, a_rows, RANK)):
-                cols = slice(piece * blocks * width, (piece + 1) * blocks * width)
-                nc.sync.dma_start(
-                    out=sb[pair][piece][:].rearrange("p (i c) -> p i c", i=PAIR), in_=dram[:, rows, cols]
-                )
+        def load_rows(sb, dram, width, pair, piece):
+            first, blocks, tile = sb[pair][piece]
+            nc.sync.dma_start(
+                out=tile[:].rearrange("p (i c) -> p i c", i=PAIR),
+                in_=dram[:, PAIR * pair : PAIR * (pair + 1), first * width : (first + blocks) * width],
+            )
+
+        def load_x(pair, piece):
+            load_rows(x_sb, x_rows, MUL, pair, piece)
+
+        def load_a(pair, piece):
+            load_rows(a_sb, a_rows, RANK, pair, piece)
 
         def block_of(sb, pair, i, j, width):
-            blocks = BLOCKS // pieces(pair)
-            return sb[pair][j // blocks], (i * blocks + j % blocks) * width
+            for first, blocks, tile in sb[pair]:
+                if first <= j < first + blocks:
+                    return tile, (i * blocks + j - first) * width
 
-        def load_weights(k):
+        def load_w_base(k):
             nc.sync.dma_start(out=w_raw[k][:], in_=w_base[k, :, :].rearrange("(q t) c -> q (t c)", t=PACK))
+
+        def load_w_lora(k):
             nc.sync.dma_start(out=wb_sb[k][:], in_=w_lora_b[k, :, :])
 
-        def quantise_weights(k):
-            w_grouped = w_work.tile([P, MUL, PACK], BF16, name="w_grouped", align_bytes=64)
-            nc.vector.tensor_copy(
-                out=w_grouped[:].rearrange("q (c r) t -> q c t r", r=4),
+        def group_weights(engine, k):
+            engine.tensor_copy(
+                out=w_grouped[k][:].rearrange("q (c r) t -> q c t r", r=4),
                 in_=w_raw[k][:].rearrange("q (t c r) -> q c t r", t=PACK, r=4),
             )
+
+        def quantise_weights(k):
             nc.vector.quantize_mx(
                 out=w_codes[k][:].bitcast(FP8X4),
                 scales=w_scales[k][:],
-                in_=w_grouped[:].rearrange("q c t -> q (c t)"),
+                in_=w_grouped[k][:].rearrange("q c t -> q (c t)"),
             )
 
-        def transpose_row_tile(step, i, xt, at):
-            pair, j = place(step)
-            x_tile, first = block_of(x_sb, pair, i, j, MUL)
-            for u in range(HALVES):
-                words = slice(first // 2 + u, first // 2 + HALVES * P, HALVES)
-                nc.tensor.transpose(xt[:, i, u, :], x_tile[:].bitcast(F32)[:, words], ident_f32[:])
-            if step % GROUP == 0:
-                for later in range(GROUP):
-                    a_tile, first = block_of(a_sb, pair, i, j - later, RANK)
-                    nc.tensor.transpose(at[:, later, i, :], a_tile[:, first : first + RANK], ident_bf16[:])
-
-        load_weights(2)
-        load_rows(0, 2)
-        load_weights(1)
-        load_rows(0, 1)
-        load_weights(0)
-        load_rows(0, 0)
+        load_a(0, 0)
+        load_w_lora(2)
+        load_w_base(2)
+        load_x(0, 0)
+        load_x(0, 1)
+        load_a(0, 1)
+        load_x(0, 2)
+        load_w_lora(1)
+        load_w_base(1)
+        load_x(0, 3)
+        load_w_lora(0)
+        load_a(1, 0)
+        load_w_base(0)
         for pair in range(1, PAIRS):
-            load_rows(pair, 0)
+            if pair > 1:
+                load_a(pair, 0)
+            for piece in range(len(X_PIECES[pair])):
+                load_x(pair, piece)
 
-        make_identity(nc, ident_f32[:])
         make_identity(nc, ident_bf16[:])
+        make_identity(nc, ident_f32[:])
+        group_weights(nc.gpsimd, 1)
+        group_weights(nc.gpsimd, 0)
 
         a_t = {}
         x_codes = {}
         x_scales = {}
-        stage = None
+        stage_of = {}
 
-        at = None
-        for step in range(-WEIGHT_LEAD, STEPS):
-            ahead = step + LOOKAHEAD
-            multiply = step >= 0
-            prepare = 0 <= ahead < STEPS
-            new_group = prepare and ahead % GROUP == 0
-            if multiply:
-                pair, j = place(step)
-                k = IRREP_OF_BLOCK[j]
-                together = 1 if step >= STEPS - GROUP else GROUP
-                if j % together == together - 1:
-                    stage = stages.tile([P, PAIR, together * MUL], F32, name="stage")
-                cols = slice((j % together) * MUL, (j % together + 1) * MUL)
-            if prepare:
-                xt = xt_banks.tile([P, PAIR, HALVES, P], F32, name="xt")
-            if new_group:
+        for step in range(-A_LEAD, STEPS):
+            x_step = step + X_LEAD
+            lora_step = step + LORA_LEAD
+            a_step = step + A_LEAD
+            do_x = 0 <= x_step < STEPS
+            do_lora = 0 <= lora_step < STEPS
+            do_a = a_step < STEPS and a_step % GROUP == 0
+            do_base = step >= 0
+
+            if do_a:
+                a_group = a_step // GROUP
                 at = at_banks.tile([P, GROUP, PAIR, P], BF16, name="at")
+                for later in range(GROUP):
+                    pair, j = place(a_step + later)
+                    for i in range(PAIR):
+                        a_tile, first = block_of(a_sb, pair, i, j, RANK)
+                        nc.tensor.transpose(at[:, later, i, :], a_tile[:, first : first + RANK], ident_bf16[:])
+            if do_x:
+                xt = xt_banks.tile([P, PAIR, HALVES, P], F32, name="xt")
+                pair, j = place(x_step)
+                for i in range(PAIR):
+                    x_tile, first = block_of(x_sb, pair, i, j, MUL)
+                    for u in range(HALVES):
+                        words = slice(first // 2 + u, first // 2 + HALVES * P, HALVES)
+                        nc.tensor.transpose(xt[:, i, u, :], x_tile[:].bitcast(F32)[:, words], ident_f32[:])
 
             lora = []
+            base = []
             for i in range(PAIR):
-                if multiply:
+                if do_lora:
+                    pair, j = place(lora_step)
                     lora_ps = lora_banks.tile([P, MUL], F32, name="lora_ps")
                     nc.tensor.matmul(
                         lora_ps[:],
-                        lhsT=a_t[step // GROUP][:, step % GROUP, i, :],
-                        rhs=wb_sb[k][:],
+                        lhsT=a_t[lora_step // GROUP][:, lora_step % GROUP, i, :],
+                        rhs=wb_sb[IRREP_OF_BLOCK[j]][:],
                         start=True,
                         stop=True,
                     )
                     lora.append(lora_ps)
-                if prepare:
-                    transpose_row_tile(ahead, i, xt, at)
-
-            if multiply:
-                for i in range(PAIR):
-                    nc.scalar.mul(out=stage[:, i, cols], in_=lora[i][:], mul=LORA_FACTOR)
-            if prepare:
-                x_grouped = x_work.tile([P, PAIR * P * PACK], BF16, name="x_grouped", align_bytes=64)
-                nc.scalar.copy(
-                    out=x_grouped[:].bitcast(F32).rearrange("q (i n u) -> q i n u", i=PAIR, u=HALVES),
-                    in_=xt[:].rearrange("q i u n -> q i n u"),
-                )
-
-            base = []
-            if multiply:
-                for i in range(PAIR):
+                if do_base:
+                    pair, j = place(step)
+                    k = IRREP_OF_BLOCK[j]
                     nodes = slice(i * P, (i + 1) * P)
                     base_ps = base_banks.tile([P, MUL], F32, name="base_ps")
                     nc.tensor.matmul_mx(
@@ -201,29 +208,52 @@ def tile_loracuetlinear_pa_t_kernel(tc, x, a_lora, w_base, w_lora_b, out):
                     )
                     base.append(base_ps)
 
+            if do_x:
+                x_grouped = x_work.tile([P, PAIR * P * PACK], BF16, name="x_grouped", align_bytes=64)
+                nc.scalar.copy(
+                    out=x_grouped[:].bitcast(F32).rearrange("q (i n u) -> q i n u", i=PAIR, u=HALVES),
+                    in_=xt[:].rearrange("q i u n -> q i n u"),
+                )
+            if do_lora:
+                pair, j = place(lora_step)
+                together = 1 if lora_step >= STEPS - GROUP else GROUP
+                if j % together == together - 1:
+                    stage = stages.tile([P, PAIR, together * MUL], F32, name="stage")
+                cols = slice((j % together) * MUL, (j % together + 1) * MUL)
+                stage_of[lora_step] = (stage, cols, together)
+                for i in range(PAIR):
+                    nc.scalar.mul(out=stage[:, i, cols], in_=lora[i][:], mul=LORA_FACTOR)
+
             def finish(i):
+                tile, cols, together = stage_of[step]
                 nc.vector.scalar_tensor_tensor(
-                    out=stage[:, i, cols], in0=base[i][:], scalar=BASE_FACTOR, in1=stage[:, i, cols],
+                    out=tile[:, i, cols], in0=base[i][:], scalar=BASE_FACTOR, in1=tile[:, i, cols],
                     op0=MULT, op1=ADD,
                 )
 
-            if step + WEIGHT_LEAD in FIRST_USE:
-                quantise_weights(FIRST_USE[step + WEIGHT_LEAD])
-            if multiply:
+            if do_base:
                 finish(0)
-            if new_group:
-                a_t[ahead // GROUP] = a_ready.tile([P, GROUP, PAIR, P], BF16, name="a_t")
-                nc.vector.tensor_copy(out=a_t[ahead // GROUP][:], in_=at[:])
-            if multiply:
+            if do_a:
+                a_t[a_group] = a_ready.tile([P, GROUP, PAIR, P], BF16, name="a_t")
+                nc.vector.tensor_copy(out=a_t[a_group][:], in_=at[:])
+            if step == -A_LEAD:
+                group_weights(nc.vector, 2)
+            for k in range(IRREPS):
+                if step + WEIGHT_LEAD == FIRST_USE[k]:
+                    quantise_weights(k)
+            if do_base:
                 finish(1)
-            if prepare:
-                x_codes[ahead] = ready.tile([P, PAIR * P], U32, name="x_codes", align_bytes=64)
-                x_scales[ahead] = ready.tile([P, PAIR * P], U8, name="x_scales", align_bytes=64)
+            if do_x:
+                x_codes[x_step] = ready.tile([P, PAIR * P], U32, name="x_codes", align_bytes=64)
+                x_scales[x_step] = ready.tile([P, PAIR * P], U8, name="x_scales", align_bytes=64)
                 nc.vector.quantize_mx(
-                    out=x_codes[ahead][:].bitcast(FP8X4), scales=x_scales[ahead][:], in_=x_grouped[:]
+                    out=x_codes[x_step][:].bitcast(FP8X4), scales=x_scales[x_step][:], in_=x_grouped[:]
                 )
 
-            if multiply and j % together == 0:
-                nc.sync.dma_start(
-                    out=out_rows[:, PAIR * pair : PAIR * (pair + 1), j * MUL : (j + together) * MUL], in_=stage[:]
-                )
+            if do_base:
+                pair, j = place(step)
+                tile, cols, together = stage_of[step]
+                if j % together == 0:
+                    nc.sync.dma_start(
+                        out=out_rows[:, PAIR * pair : PAIR * (pair + 1), j * MUL : (j + together) * MUL], in_=tile[:]
+                    )

@@ -32,9 +32,11 @@ STEPS = PAIRS * BLOCKS
 HALVES = 2
 GROUP = 3
 X_LEAD = 2
-LORA_LEAD = 3
-A_LEAD = 5
+LORA_LEAD = 0
+A_LEAD = 3
+GROUP_WEIGHTS_LEAD = 5
 WEIGHT_LEAD = 2
+FIRST_LEAD = max(X_LEAD, LORA_LEAD, A_LEAD, GROUP_WEIGHTS_LEAD, WEIGHT_LEAD)
 STAGE_BUFS = 7
 X_PIECES = ((1, 2, 3, 3), (3, 6), (9,), (9,))
 A_PIECES = ((3, 6), (9,), (9,), (9,))
@@ -110,8 +112,8 @@ def tile_loracuetlinear_pa_t_kernel(tc, x, a_lora, w_base, w_lora_b, out):
         def load_w_lora(k):
             nc.sync.dma_start(out=wb_sb[k][:], in_=w_lora_b[k, :, :])
 
-        def group_weights(engine, k):
-            engine.tensor_copy(
+        def group_weights(k):
+            nc.vector.tensor_copy(
                 out=w_grouped[k][:].rearrange("q (c r) t -> q c t r", r=4),
                 in_=w_raw[k][:].rearrange("q (t c r) -> q c t r", t=PACK, r=4),
             )
@@ -144,40 +146,40 @@ def tile_loracuetlinear_pa_t_kernel(tc, x, a_lora, w_base, w_lora_b, out):
 
         make_identity(nc, ident_bf16[:])
         make_identity(nc, ident_f32[:])
-        group_weights(nc.gpsimd, 1)
-        group_weights(nc.gpsimd, 0)
 
         a_t = {}
         x_codes = {}
         x_scales = {}
         stage_of = {}
 
-        for step in range(-A_LEAD, STEPS):
+        for step in range(-FIRST_LEAD, STEPS):
             x_step = step + X_LEAD
             lora_step = step + LORA_LEAD
             a_step = step + A_LEAD
             do_x = 0 <= x_step < STEPS
             do_lora = 0 <= lora_step < STEPS
-            do_a = a_step < STEPS and a_step % GROUP == 0
+            do_a = 0 <= a_step < STEPS and a_step % GROUP == 0
             do_base = step >= 0
 
-            if do_a:
-                a_group = a_step // GROUP
-                at = at_banks.tile([P, GROUP, PAIR, P], BF16, name="at")
+            def transpose_x(i):
+                pair, j = place(x_step)
+                x_tile, first = block_of(x_sb, pair, i, j, MUL)
+                for u in range(HALVES):
+                    words = slice(first // 2 + u, first // 2 + HALVES * P, HALVES)
+                    nc.tensor.transpose(xt[:, i, u, :], x_tile[:].bitcast(F32)[:, words], ident_f32[:])
+
+            def transpose_a():
                 for later in range(GROUP):
                     pair, j = place(a_step + later)
                     for i in range(PAIR):
                         a_tile, first = block_of(a_sb, pair, i, j, RANK)
                         nc.tensor.transpose(at[:, later, i, :], a_tile[:, first : first + RANK], ident_bf16[:])
+
             if do_x:
                 xt = xt_banks.tile([P, PAIR, HALVES, P], F32, name="xt")
-                pair, j = place(x_step)
-                for i in range(PAIR):
-                    x_tile, first = block_of(x_sb, pair, i, j, MUL)
-                    for u in range(HALVES):
-                        words = slice(first // 2 + u, first // 2 + HALVES * P, HALVES)
-                        nc.tensor.transpose(xt[:, i, u, :], x_tile[:].bitcast(F32)[:, words], ident_f32[:])
-
+            if do_a:
+                a_group = a_step // GROUP
+                at = at_banks.tile([P, GROUP, PAIR, P], BF16, name="at")
             lora = []
             base = []
             for i in range(PAIR):
@@ -192,9 +194,14 @@ def tile_loracuetlinear_pa_t_kernel(tc, x, a_lora, w_base, w_lora_b, out):
                         stop=True,
                     )
                     lora.append(lora_ps)
-                if do_base:
-                    pair, j = place(step)
-                    k = IRREP_OF_BLOCK[j]
+                if do_a and i == PAIR - 1:
+                    transpose_a()
+                if do_x:
+                    transpose_x(i)
+            if do_base:
+                pair, j = place(step)
+                k = IRREP_OF_BLOCK[j]
+                for i in range(PAIR):
                     nodes = slice(i * P, (i + 1) * P)
                     base_ps = base_banks.tile([P, MUL], F32, name="base_ps")
                     nc.tensor.matmul_mx(
@@ -208,12 +215,6 @@ def tile_loracuetlinear_pa_t_kernel(tc, x, a_lora, w_base, w_lora_b, out):
                     )
                     base.append(base_ps)
 
-            if do_x:
-                x_grouped = x_work.tile([P, PAIR * P * PACK], BF16, name="x_grouped", align_bytes=64)
-                nc.scalar.copy(
-                    out=x_grouped[:].bitcast(F32).rearrange("q (i n u) -> q i n u", i=PAIR, u=HALVES),
-                    in_=xt[:].rearrange("q i u n -> q i n u"),
-                )
             if do_lora:
                 pair, j = place(lora_step)
                 together = 1 if lora_step >= STEPS - GROUP else GROUP
@@ -224,6 +225,13 @@ def tile_loracuetlinear_pa_t_kernel(tc, x, a_lora, w_base, w_lora_b, out):
                 for i in range(PAIR):
                     nc.scalar.mul(out=stage[:, i, cols], in_=lora[i][:], mul=LORA_FACTOR)
 
+            if do_x:
+                x_grouped = x_work.tile([P, PAIR * P * PACK], BF16, name="x_grouped", align_bytes=64)
+                nc.scalar.copy(
+                    out=x_grouped[:].bitcast(F32).rearrange("q (i n u) -> q i n u", i=PAIR, u=HALVES),
+                    in_=xt[:].rearrange("q i u n -> q i n u"),
+                )
+
             def finish(i):
                 tile, cols, together = stage_of[step]
                 nc.vector.scalar_tensor_tensor(
@@ -231,17 +239,11 @@ def tile_loracuetlinear_pa_t_kernel(tc, x, a_lora, w_base, w_lora_b, out):
                     op0=MULT, op1=ADD,
                 )
 
-            if do_base:
-                finish(0)
             if do_a:
                 a_t[a_group] = a_ready.tile([P, GROUP, PAIR, P], BF16, name="a_t")
                 nc.vector.tensor_copy(out=a_t[a_group][:], in_=at[:])
-            if step == -A_LEAD:
-                group_weights(nc.vector, 2)
-            for k in range(IRREPS):
-                if step + WEIGHT_LEAD == FIRST_USE[k]:
-                    quantise_weights(k)
             if do_base:
+                finish(0)
                 finish(1)
             if do_x:
                 x_codes[x_step] = ready.tile([P, PAIR * P], U32, name="x_codes", align_bytes=64)
@@ -249,6 +251,12 @@ def tile_loracuetlinear_pa_t_kernel(tc, x, a_lora, w_base, w_lora_b, out):
                 nc.vector.quantize_mx(
                     out=x_codes[x_step][:].bitcast(FP8X4), scales=x_scales[x_step][:], in_=x_grouped[:]
                 )
+            for k in range(IRREPS):
+                if step + GROUP_WEIGHTS_LEAD == FIRST_USE[k]:
+                    group_weights(k)
+            for k in range(IRREPS):
+                if step + WEIGHT_LEAD == FIRST_USE[k]:
+                    quantise_weights(k)
 
             if do_base:
                 pair, j = place(step)

@@ -32,8 +32,8 @@ STEPS = PAIRS * BLOCKS
 HALVES = 2
 GROUP = 3
 X_LEAD = 2
-LORA_LEAD = 0
-A_LEAD = 3
+LORA_LEAD = 1
+A_LEAD = 4
 GROUP_WEIGHTS_LEAD = 5
 WEIGHT_LEAD = 2
 FIRST_LEAD = max(X_LEAD, LORA_LEAD, A_LEAD, GROUP_WEIGHTS_LEAD, WEIGHT_LEAD)
@@ -161,6 +161,18 @@ def tile_loracuetlinear_pa_t_kernel(tc, x, a_lora, w_base, w_lora_b, out):
             do_a = 0 <= a_step < STEPS and a_step % GROUP == 0
             do_base = step >= 0
 
+            if do_x:
+                xt = xt_banks.tile([P, PAIR, HALVES, P], F32, name="xt")
+                x_grouped = x_work.tile([P, PAIR * P * PACK], BF16, name="x_grouped", align_bytes=64)
+                x_codes[x_step] = ready.tile([P, PAIR * P], U32, name="x_codes", align_bytes=64)
+                x_scales[x_step] = ready.tile([P, PAIR * P], U8, name="x_scales", align_bytes=64)
+            if do_a:
+                a_group = a_step // GROUP
+                at = at_banks.tile([P, GROUP, PAIR, P], BF16, name="at")
+                a_t[a_group] = a_ready.tile([P, GROUP, PAIR, P], BF16, name="a_t")
+            lora = {}
+            base = {}
+
             def transpose_x(i):
                 pair, j = place(x_step)
                 x_tile, first = block_of(x_sb, pair, i, j, MUL)
@@ -175,61 +187,45 @@ def tile_loracuetlinear_pa_t_kernel(tc, x, a_lora, w_base, w_lora_b, out):
                         a_tile, first = block_of(a_sb, pair, i, j, RANK)
                         nc.tensor.transpose(at[:, later, i, :], a_tile[:, first : first + RANK], ident_bf16[:])
 
-            if do_x:
-                xt = xt_banks.tile([P, PAIR, HALVES, P], F32, name="xt")
-            if do_a:
-                a_group = a_step // GROUP
-                at = at_banks.tile([P, GROUP, PAIR, P], BF16, name="at")
-            lora = []
-            base = []
-            for i in range(PAIR):
-                if do_lora:
-                    pair, j = place(lora_step)
-                    lora_ps = lora_banks.tile([P, MUL], F32, name="lora_ps")
-                    nc.tensor.matmul(
-                        lora_ps[:],
-                        lhsT=a_t[lora_step // GROUP][:, lora_step % GROUP, i, :],
-                        rhs=wb_sb[IRREP_OF_BLOCK[j]][:],
-                        start=True,
-                        stop=True,
-                    )
-                    lora.append(lora_ps)
-                if do_a and i == PAIR - 1:
-                    transpose_a()
-                if do_x:
-                    transpose_x(i)
-            if do_base:
+            def multiply_lora(i):
+                pair, j = place(lora_step)
+                lora[i] = lora_banks.tile([P, MUL], F32, name="lora_ps")
+                nc.tensor.matmul(
+                    lora[i][:],
+                    lhsT=a_t[lora_step // GROUP][:, lora_step % GROUP, i, :],
+                    rhs=wb_sb[IRREP_OF_BLOCK[j]][:],
+                    start=True,
+                    stop=True,
+                )
+
+            def multiply_base(i):
                 pair, j = place(step)
                 k = IRREP_OF_BLOCK[j]
-                for i in range(PAIR):
-                    nodes = slice(i * P, (i + 1) * P)
-                    base_ps = base_banks.tile([P, MUL], F32, name="base_ps")
-                    nc.tensor.matmul_mx(
-                        out=base_ps[:],
-                        lhsT=x_codes[step][:, nodes].bitcast(FP8X4),
-                        lhsT_scale=x_scales[step][:, nodes],
-                        rhs=w_codes[k][:].bitcast(FP8X4),
-                        rhs_scale=w_scales[k][:],
-                        start=True,
-                        stop=True,
-                    )
-                    base.append(base_ps)
+                nodes = slice(i * P, (i + 1) * P)
+                base[i] = base_banks.tile([P, MUL], F32, name="base_ps")
+                nc.tensor.matmul_mx(
+                    out=base[i][:],
+                    lhsT=x_codes[step][:, nodes].bitcast(FP8X4),
+                    lhsT_scale=x_scales[step][:, nodes],
+                    rhs=w_codes[k][:].bitcast(FP8X4),
+                    rhs_scale=w_scales[k][:],
+                    start=True,
+                    stop=True,
+                )
 
-            if do_lora:
-                pair, j = place(lora_step)
-                together = 1 if lora_step >= STEPS - GROUP else GROUP
-                if j % together == together - 1:
-                    stage = stages.tile([P, PAIR, together * MUL], F32, name="stage")
-                cols = slice((j % together) * MUL, (j % together + 1) * MUL)
-                stage_of[lora_step] = (stage, cols, together)
-                for i in range(PAIR):
-                    nc.scalar.mul(out=stage[:, i, cols], in_=lora[i][:], mul=LORA_FACTOR)
+            def scale_lora(i):
+                tile, cols, together = stage_of[lora_step]
+                nc.scalar.mul(out=tile[:, i, cols], in_=lora[i][:], mul=LORA_FACTOR)
 
-            if do_x:
-                x_grouped = x_work.tile([P, PAIR * P * PACK], BF16, name="x_grouped", align_bytes=64)
+            def group_x():
                 nc.scalar.copy(
                     out=x_grouped[:].bitcast(F32).rearrange("q (i n u) -> q i n u", i=PAIR, u=HALVES),
                     in_=xt[:].rearrange("q i u n -> q i n u"),
+                )
+
+            def quantise_x():
+                nc.vector.quantize_mx(
+                    out=x_codes[x_step][:].bitcast(FP8X4), scales=x_scales[x_step][:], in_=x_grouped[:]
                 )
 
             def finish(i):
@@ -239,25 +235,44 @@ def tile_loracuetlinear_pa_t_kernel(tc, x, a_lora, w_base, w_lora_b, out):
                     op0=MULT, op1=ADD,
                 )
 
+            if do_lora:
+                pair, j = place(lora_step)
+                together = 1 if lora_step >= STEPS - GROUP else GROUP
+                if j % together == together - 1:
+                    stage = stages.tile([P, PAIR, together * MUL], F32, name="stage")
+                stage_of[lora_step] = (stage, slice((j % together) * MUL, (j % together + 1) * MUL), together)
+
+            if do_lora:
+                multiply_lora(0)
+            if do_x:
+                transpose_x(0)
+            if do_lora:
+                multiply_lora(1)
             if do_a:
-                a_t[a_group] = a_ready.tile([P, GROUP, PAIR, P], BF16, name="a_t")
-                nc.vector.tensor_copy(out=a_t[a_group][:], in_=at[:])
+                transpose_a()
+            if do_x:
+                transpose_x(1)
+            if do_base:
+                multiply_base(0)
+                multiply_base(1)
+            if do_lora:
+                scale_lora(0)
+                scale_lora(1)
+            if do_x:
+                group_x()
             if do_base:
                 finish(0)
                 finish(1)
+            if do_a:
+                nc.vector.tensor_copy(out=a_t[a_group][:], in_=at[:])
             if do_x:
-                x_codes[x_step] = ready.tile([P, PAIR * P], U32, name="x_codes", align_bytes=64)
-                x_scales[x_step] = ready.tile([P, PAIR * P], U8, name="x_scales", align_bytes=64)
-                nc.vector.quantize_mx(
-                    out=x_codes[x_step][:].bitcast(FP8X4), scales=x_scales[x_step][:], in_=x_grouped[:]
-                )
+                quantise_x()
             for k in range(IRREPS):
                 if step + GROUP_WEIGHTS_LEAD == FIRST_USE[k]:
                     group_weights(k)
             for k in range(IRREPS):
                 if step + WEIGHT_LEAD == FIRST_USE[k]:
                     quantise_weights(k)
-
             if do_base:
                 pair, j = place(step)
                 tile, cols, together = stage_of[step]

@@ -20,26 +20,27 @@ RANK = 128
 IRREP_OF_BLOCK = (0, 1, 1, 1, 2, 2, 2, 2, 2)
 BLOCKS = len(IRREP_OF_BLOCK)
 IRREPS = 3
-FIRST_USE = {
-    IRREP_OF_BLOCK[j]: BLOCKS - 1 - j
-    for j in range(BLOCKS)
-    if j == BLOCKS - 1 or IRREP_OF_BLOCK[j + 1] != IRREP_OF_BLOCK[j]
-}
 ROW_TILES = NODES // P
 PAIR = 2
 PAIRS = ROW_TILES // PAIR
 STEPS = PAIRS * BLOCKS
 HALVES = 2
 GROUP = 3
+GROUPS = [(0, 0), (1, 0)] + [
+    (pair, number) for pair in range(PAIRS) for number in range(BLOCKS // GROUP) if number > 0 or pair > 1
+]
+PLACES = [(pair, BLOCKS - 1 - GROUP * number - later) for pair, number in GROUPS for later in range(GROUP)]
+FIRST_USE = [min(step for step, (pair, j) in enumerate(PLACES) if IRREP_OF_BLOCK[j] == k) for k in range(IRREPS)]
 X_LEAD = 2
 LORA_LEAD = 1
 A_LEAD = 4
-GROUP_WEIGHTS_LEAD = 5
+GROUP_WEIGHTS_LEAD = 7
+WEIGHT_PARTS = 4
 WEIGHT_LEAD = 2
 FIRST_LEAD = max(X_LEAD, LORA_LEAD, A_LEAD, GROUP_WEIGHTS_LEAD, WEIGHT_LEAD)
 STAGE_BUFS = 7
-X_PIECES = ((1, 2, 3, 3), (3, 6), (9,), (9,))
-A_PIECES = ((3, 6), (9,), (9,), (9,))
+X_PIECES = ((1, 1, 1, 3, 3), (3, 6), (9,), (9,))
+A_PIECES = ((3, 6), (3, 6), (9,), (9,))
 
 BASE_FACTOR = 1.0 / math.sqrt(MUL)
 LORA_FACTOR = 2.0 / math.sqrt(RANK)
@@ -80,13 +81,10 @@ def tile_loracuetlinear_pa_t_kernel(tc, x, a_lora, w_base, w_lora_b, out):
         w_grouped = [keep.tile([P, MUL, PACK], BF16, name="w_grouped%d" % k, align_bytes=64) for k in range(IRREPS)]
         w_codes = [keep.tile([P, MUL], U32, name="w_codes%d" % k, align_bytes=64) for k in range(IRREPS)]
         w_scales = [keep.tile([P, MUL], U8, name="w_scales%d" % k, align_bytes=64) for k in range(IRREPS)]
+        fence = keep.tile([P, 1], U32, name="fence")
         wb_sb = [keep.tile([P, MUL], BF16, name="wb_sb%d" % k) for k in range(IRREPS)]
         ident_f32 = keep.tile([P, P], F32, name="ident_f32")
         ident_bf16 = keep.tile([P, P], BF16, name="ident_bf16")
-
-        def place(step):
-            pair, position = divmod(step, BLOCKS)
-            return pair, BLOCKS - 1 - position
 
         def load_rows(sb, dram, width, pair, piece):
             first, blocks, tile = sb[pair][piece]
@@ -118,6 +116,15 @@ def tile_loracuetlinear_pa_t_kernel(tc, x, a_lora, w_base, w_lora_b, out):
                 in_=w_raw[k][:].rearrange("q (t c r) -> q c t r", t=PACK, r=4),
             )
 
+        def group_weights_part(k, part, after):
+            nc.gpsimd.tensor_copy(out=fence[:], in_=after[:, :1])
+            cols = slice(part * MUL // WEIGHT_PARTS, (part + 1) * MUL // WEIGHT_PARTS)
+            nc.gpsimd.tensor_scalar(
+                out=w_grouped[k][:, cols, :].rearrange("q (c r) t -> q c t r", r=4),
+                in0=w_raw[k][:].rearrange("q (t c) -> q t c", t=PACK)[:, :, cols].rearrange("q t (c r) -> q c t r", r=4),
+                scalar1=1.0, scalar2=0.0, op0=MULT, op1=ADD,
+            )
+
         def quantise_weights(k):
             nc.vector.quantize_mx(
                 out=w_codes[k][:].bitcast(FP8X4),
@@ -125,24 +132,26 @@ def tile_loracuetlinear_pa_t_kernel(tc, x, a_lora, w_base, w_lora_b, out):
                 in_=w_grouped[k][:].rearrange("q c t -> q (c t)"),
             )
 
+        load_w_base(2)
         load_a(0, 0)
         load_w_lora(2)
-        load_w_base(2)
         load_x(0, 0)
+        load_a(1, 0)
         load_x(0, 1)
-        load_a(0, 1)
         load_x(0, 2)
+        load_x(1, 0)
+        load_a(0, 1)
+        load_x(0, 3)
         load_w_lora(1)
         load_w_base(1)
-        load_x(0, 3)
+        load_x(0, 4)
         load_w_lora(0)
-        load_a(1, 0)
         load_w_base(0)
-        for pair in range(1, PAIRS):
-            if pair > 1:
-                load_a(pair, 0)
-            for piece in range(len(X_PIECES[pair])):
-                load_x(pair, piece)
+        load_a(1, 1)
+        load_x(1, 1)
+        for pair in range(2, PAIRS):
+            load_a(pair, 0)
+            load_x(pair, 0)
 
         make_identity(nc, ident_bf16[:])
         make_identity(nc, ident_f32[:])
@@ -174,7 +183,7 @@ def tile_loracuetlinear_pa_t_kernel(tc, x, a_lora, w_base, w_lora_b, out):
             base = {}
 
             def transpose_x(i):
-                pair, j = place(x_step)
+                pair, j = PLACES[x_step]
                 x_tile, first = block_of(x_sb, pair, i, j, MUL)
                 for u in range(HALVES):
                     words = slice(first // 2 + u, first // 2 + HALVES * P, HALVES)
@@ -182,13 +191,13 @@ def tile_loracuetlinear_pa_t_kernel(tc, x, a_lora, w_base, w_lora_b, out):
 
             def transpose_a():
                 for later in range(GROUP):
-                    pair, j = place(a_step + later)
+                    pair, j = PLACES[a_step + later]
                     for i in range(PAIR):
                         a_tile, first = block_of(a_sb, pair, i, j, RANK)
                         nc.tensor.transpose(at[:, later, i, :], a_tile[:, first : first + RANK], ident_bf16[:])
 
             def multiply_lora(i):
-                pair, j = place(lora_step)
+                pair, j = PLACES[lora_step]
                 lora[i] = lora_banks.tile([P, MUL], F32, name="lora_ps")
                 nc.tensor.matmul(
                     lora[i][:],
@@ -199,7 +208,7 @@ def tile_loracuetlinear_pa_t_kernel(tc, x, a_lora, w_base, w_lora_b, out):
                 )
 
             def multiply_base(i):
-                pair, j = place(step)
+                pair, j = PLACES[step]
                 k = IRREP_OF_BLOCK[j]
                 nodes = slice(i * P, (i + 1) * P)
                 base[i] = base_banks.tile([P, MUL], F32, name="base_ps")
@@ -236,12 +245,16 @@ def tile_loracuetlinear_pa_t_kernel(tc, x, a_lora, w_base, w_lora_b, out):
                 )
 
             if do_lora:
-                pair, j = place(lora_step)
+                pair, j = PLACES[lora_step]
                 together = 1 if lora_step >= STEPS - GROUP else GROUP
                 if j % together == together - 1:
                     stage = stages.tile([P, PAIR, together * MUL], F32, name="stage")
                 stage_of[lora_step] = (stage, slice((j % together) * MUL, (j % together + 1) * MUL), together)
 
+            for k in range(IRREPS):
+                part = step + GROUP_WEIGHTS_LEAD - FIRST_USE[k]
+                if FIRST_USE[k] > 0 and 0 <= part < WEIGHT_PARTS:
+                    group_weights_part(k, part, x_codes[x_step - 1])
             if do_lora:
                 multiply_lora(0)
             if do_x:
@@ -260,23 +273,26 @@ def tile_loracuetlinear_pa_t_kernel(tc, x, a_lora, w_base, w_lora_b, out):
                 scale_lora(1)
             if do_x:
                 group_x()
+            if do_a:
+                nc.vector.tensor_copy(out=a_t[a_group][:], in_=at[:])
             if do_base:
                 finish(0)
                 finish(1)
-            if do_a:
-                nc.vector.tensor_copy(out=a_t[a_group][:], in_=at[:])
             if do_x:
                 quantise_x()
-            for k in range(IRREPS):
-                if step + GROUP_WEIGHTS_LEAD == FIRST_USE[k]:
-                    group_weights(k)
+            if step == FIRST_USE[IRREP_OF_BLOCK[BLOCKS - 1]] - FIRST_LEAD:
+                group_weights(IRREP_OF_BLOCK[BLOCKS - 1])
             for k in range(IRREPS):
                 if step + WEIGHT_LEAD == FIRST_USE[k]:
                     quantise_weights(k)
             if do_base:
-                pair, j = place(step)
+                pair, j = PLACES[step]
                 tile, cols, together = stage_of[step]
+                parts = PAIR if step == STEPS - 1 else 1
                 if j % together == 0:
-                    nc.sync.dma_start(
-                        out=out_rows[:, PAIR * pair : PAIR * (pair + 1), j * MUL : (j + together) * MUL], in_=tile[:]
-                    )
+                    for part in range(parts):
+                        rows = slice(part * PAIR // parts, (part + 1) * PAIR // parts)
+                        nc.sync.dma_start(
+                            out=out_rows[:, PAIR * pair + rows.start : PAIR * pair + rows.stop, j * MUL : (j + together) * MUL],
+                            in_=tile[:, rows, :],
+                        )

@@ -36,9 +36,11 @@ LORA_LEAD = 1
 A_LEAD = 4
 GROUP_WEIGHTS_LEAD = 7
 WEIGHT_PARTS = 4
+PERMUTE_LEAD = X_LEAD + 1
 WEIGHT_LEAD = 2
 FIRST_LEAD = max(X_LEAD, LORA_LEAD, A_LEAD, GROUP_WEIGHTS_LEAD, WEIGHT_LEAD)
 STAGE_BUFS = 7
+PERMUTE_FROM = 15
 X_PIECES = ((1, 1, 1, 3, 3), (3, 6), (9,), (9,))
 A_PIECES = ((3, 6), (3, 6), (9,), (9,))
 
@@ -56,7 +58,7 @@ def tile_loracuetlinear_pa_t_kernel(tc, x, a_lora, w_base, w_lora_b, out):
 
     with ExitStack() as ctx:
         keep = ctx.enter_context(tc.tile_pool(name="keep", bufs=1))
-        x_work = ctx.enter_context(tc.tile_pool(name="x_work", bufs=3))
+        x_work = ctx.enter_context(tc.tile_pool(name="x_work", bufs=5))
         ready = ctx.enter_context(tc.tile_pool(name="ready", bufs=X_LEAD + 2))
         a_ready = ctx.enter_context(tc.tile_pool(name="a_ready", bufs=4))
         stages = ctx.enter_context(tc.tile_pool(name="stages", bufs=STAGE_BUFS))
@@ -99,10 +101,14 @@ def tile_loracuetlinear_pa_t_kernel(tc, x, a_lora, w_base, w_lora_b, out):
         def load_a(pair, piece):
             load_rows(a_sb, a_rows, RANK, pair, piece)
 
-        def block_of(sb, pair, i, j, width):
+        def piece_of(sb, pair, j):
             for first, blocks, tile in sb[pair]:
                 if first <= j < first + blocks:
-                    return tile, (i * blocks + j - first) * width
+                    return first, blocks, tile
+
+        def block_of(sb, pair, i, j, width):
+            first, blocks, tile = piece_of(sb, pair, j)
+            return tile, (i * blocks + j - first) * width
 
         def load_w_base(k):
             nc.sync.dma_start(out=w_raw[k][:], in_=w_base[k, :, :].rearrange("(q t) c -> q (t c)", t=PACK))
@@ -159,6 +165,7 @@ def tile_loracuetlinear_pa_t_kernel(tc, x, a_lora, w_base, w_lora_b, out):
         a_t = {}
         x_codes = {}
         x_scales = {}
+        x_words = {}
         stage_of = {}
 
         for step in range(-FIRST_LEAD, STEPS):
@@ -167,14 +174,18 @@ def tile_loracuetlinear_pa_t_kernel(tc, x, a_lora, w_base, w_lora_b, out):
             a_step = step + A_LEAD
             do_x = 0 <= x_step < STEPS
             do_lora = 0 <= lora_step < STEPS
+            p_step = step + PERMUTE_LEAD
+            do_p = PERMUTE_FROM <= p_step < STEPS
             do_a = 0 <= a_step < STEPS and a_step % GROUP == 0
             do_base = step >= 0
 
             if do_x:
                 xt = xt_banks.tile([P, PAIR, HALVES, P], F32, name="xt")
-                x_grouped = x_work.tile([P, PAIR * P * PACK], BF16, name="x_grouped", align_bytes=64)
+                x_grouped = x_work.tile([P, PAIR * P * PACK], BF16, name="x_part", align_bytes=64)
                 x_codes[x_step] = ready.tile([P, PAIR * P], U32, name="x_codes", align_bytes=64)
                 x_scales[x_step] = ready.tile([P, PAIR * P], U8, name="x_scales", align_bytes=64)
+            if do_p:
+                x_words[p_step] = x_work.tile([P, P * PACK], BF16, name="x_part", align_bytes=64)
             if do_a:
                 a_group = a_step // GROUP
                 at = at_banks.tile([P, GROUP, PAIR, P], BF16, name="at")
@@ -186,8 +197,21 @@ def tile_loracuetlinear_pa_t_kernel(tc, x, a_lora, w_base, w_lora_b, out):
                 pair, j = PLACES[x_step]
                 x_tile, first = block_of(x_sb, pair, i, j, MUL)
                 for u in range(HALVES):
-                    words = slice(first // 2 + u, first // 2 + HALVES * P, HALVES)
-                    nc.tensor.transpose(xt[:, i, u, :], x_tile[:].bitcast(F32)[:, words], ident_f32[:])
+                    if u == 1 and x_step in x_words:
+                        words = x_words[x_step][:].bitcast(F32)[:, i * P : (i + 1) * P]
+                    else:
+                        words = x_tile[:].bitcast(F32)[:, first // 2 + u : first // 2 + HALVES * P : HALVES]
+                    nc.tensor.transpose(xt[:, i, u, :], words, ident_f32[:])
+
+            def permute_x():
+                pair, j = PLACES[p_step]
+                first, blocks, x_tile = piece_of(x_sb, pair, j)
+                words = x_tile[:].rearrange("p (i b q u e) -> p i b q u e", i=PAIR, b=blocks, u=HALVES, e=2)
+                nc.gpsimd.tensor_scalar(
+                    out=x_words[p_step][:].rearrange("p (i q e) -> p i q e", i=PAIR, e=2),
+                    in0=words[:, :, j - first, :, 1, :],
+                    scalar1=1.0, scalar2=0.0, op0=MULT, op1=ADD,
+                )
 
             def transpose_a():
                 for later in range(GROUP):
@@ -255,16 +279,18 @@ def tile_loracuetlinear_pa_t_kernel(tc, x, a_lora, w_base, w_lora_b, out):
                 part = step + GROUP_WEIGHTS_LEAD - FIRST_USE[k]
                 if FIRST_USE[k] > 0 and 0 <= part < WEIGHT_PARTS:
                     group_weights_part(k, part, x_codes[x_step - 1])
+            if do_p:
+                permute_x()
             if do_lora:
                 multiply_lora(0)
             if do_x:
                 transpose_x(0)
             if do_lora:
                 multiply_lora(1)
-            if do_a:
-                transpose_a()
             if do_x:
                 transpose_x(1)
+            if do_a:
+                transpose_a()
             if do_base:
                 multiply_base(0)
                 multiply_base(1)

import math
from contextlib import ExitStack

import concourse.mybir as mybir
from concourse.masks import make_identity

F32 = mybir.dt.float32
BF16 = mybir.dt.bfloat16
U32 = mybir.dt.uint32
U8 = mybir.dt.uint8
FP8X4 = mybir.dt.float8_e4m3fn_x4
MULT = mybir.AluOpType.mult
ADD = mybir.AluOpType.add

P = 128
PACK = 4
NODES = 1024
MUL = 512
RANK = 128
IRREP_OF_BLOCK = (0, 1, 1, 1, 2, 2, 2, 2, 2)
BLOCKS = len(IRREP_OF_BLOCK)
IRREPS = 3
ROW_TILES = NODES // P
PAIR = 2
PAIRS = ROW_TILES // PAIR
STEPS = PAIRS * BLOCKS
HALVES = 2
GROUP = 3
GROUPS = [(0, 0), (1, 0)] + [
    (pair, number) for pair in range(PAIRS) for number in range(BLOCKS // GROUP) if number > 0 or pair > 1
]
PLACES = [(pair, BLOCKS - 1 - GROUP * number - later) for pair, number in GROUPS for later in range(GROUP)]
FIRST_USE = [min(step for step, (pair, j) in enumerate(PLACES) if IRREP_OF_BLOCK[j] == k) for k in range(IRREPS)]
X_LEAD = 2
LORA_LEAD = 1
A_LEAD = 4
GROUP_WEIGHTS_LEAD = 7
WEIGHT_PARTS = 4
PERMUTE_LEAD = X_LEAD + 1
WEIGHT_LEAD = 2
FIRST_LEAD = max(X_LEAD, LORA_LEAD, A_LEAD, GROUP_WEIGHTS_LEAD, WEIGHT_LEAD)
STAGE_BUFS = 7
PERMUTE_FROM = 15
X_PIECES = ((1, 1, 1, 3, 3), (3, 6), (9,), (9,))
A_PIECES = ((3, 6), (3, 6), (9,), (9,))

BASE_FACTOR = 1.0 / math.sqrt(MUL)
LORA_FACTOR = 2.0 / math.sqrt(RANK)

FLOPS = 2 * NODES * BLOCKS * MUL * (MUL + RANK)


def tile_loracuetlinear_pa_t_kernel(tc, x, a_lora, w_base, w_lora_b, out):
    nc = tc.nc
    x_rows = x.rearrange("(p r) c -> p r c", r=ROW_TILES)
    a_rows = a_lora.rearrange("(p r) c -> p r c", r=ROW_TILES)
    out_rows = out.rearrange("(p r) c -> p r c", r=ROW_TILES)

    with ExitStack() as ctx:
        keep = ctx.enter_context(tc.tile_pool(name="keep", bufs=1))
        x_work = ctx.enter_context(tc.tile_pool(name="x_work", bufs=5))
        ready = ctx.enter_context(tc.tile_pool(name="ready", bufs=X_LEAD + 2))
        a_ready = ctx.enter_context(tc.tile_pool(name="a_ready", bufs=4))
        stages = ctx.enter_context(tc.tile_pool(name="stages", bufs=STAGE_BUFS))
        xt_banks = ctx.enter_context(tc.psum_pool(name="xt_banks", bufs=2))
        at_banks = ctx.enter_context(tc.psum_pool(name="at_banks", bufs=1))
        lora_banks = ctx.enter_context(tc.psum_pool(name="lora_banks", bufs=2))
        base_banks = ctx.enter_context(tc.psum_pool(name="base_banks", bufs=3))
        ctx.enter_context(tc.manual_schedule())

        def cut(pieces, name, width):
            top = BLOCKS
            tiles = []
            for blocks in pieces:
                top -= blocks
                tile = keep.tile([P, PAIR * blocks * width], BF16, name="%s_%d" % (name, top))
                tiles.append((top, blocks, tile))
            return tiles

        x_sb = [cut(X_PIECES[pair], "x%d" % pair, MUL) for pair in range(PAIRS)]
        a_sb = [cut(A_PIECES[pair], "a%d" % pair, RANK) for pair in range(PAIRS)]
        w_raw = [keep.tile([P, PACK * MUL], BF16, name="w_raw%d" % k) for k in range(IRREPS)]
        w_grouped = [keep.tile([P, MUL, PACK], BF16, name="w_grouped%d" % k, align_bytes=64) for k in range(IRREPS)]
        w_codes = [keep.tile([P, MUL], U32, name="w_codes%d" % k, align_bytes=64) for k in range(IRREPS)]
        w_scales = [keep.tile([P, MUL], U8, name="w_scales%d" % k, align_bytes=64) for k in range(IRREPS)]
        fence = keep.tile([P, 1], U32, name="fence")
        wb_sb = [keep.tile([P, MUL], BF16, name="wb_sb%d" % k) for k in range(IRREPS)]
        ident_f32 = keep.tile([P, P], F32, name="ident_f32")
        ident_bf16 = keep.tile([P, P], BF16, name="ident_bf16")

        def load_rows(sb, dram, width, pair, piece):
            first, blocks, tile = sb[pair][piece]
            nc.sync.dma_start(
                out=tile[:].rearrange("p (i c) -> p i c", i=PAIR),
                in_=dram[:, PAIR * pair : PAIR * (pair + 1), first * width : (first + blocks) * width],
            )

        def load_x(pair, piece):
            load_rows(x_sb, x_rows, MUL, pair, piece)

        def load_a(pair, piece):
            load_rows(a_sb, a_rows, RANK, pair, piece)

        def piece_of(sb, pair, j):
            for first, blocks, tile in sb[pair]:
                if first <= j < first + blocks:
                    return first, blocks, tile

        def block_of(sb, pair, i, j, width):
            first, blocks, tile = piece_of(sb, pair, j)
            return tile, (i * blocks + j - first) * width

        def load_w_base(k):
            nc.sync.dma_start(out=w_raw[k][:], in_=w_base[k, :, :].rearrange("(q t) c -> q (t c)", t=PACK))

        def load_w_lora(k):
            nc.sync.dma_start(out=wb_sb[k][:], in_=w_lora_b[k, :, :])

        def group_weights(k):
            nc.vector.tensor_copy(
                out=w_grouped[k][:].rearrange("q (c r) t -> q c t r", r=4),
                in_=w_raw[k][:].rearrange("q (t c r) -> q c t r", t=PACK, r=4),
            )

        def group_weights_part(k, part, after):
            nc.gpsimd.tensor_copy(out=fence[:], in_=after[:, :1])
            cols = slice(part * MUL // WEIGHT_PARTS, (part + 1) * MUL // WEIGHT_PARTS)
            nc.gpsimd.tensor_scalar(
                out=w_grouped[k][:, cols, :].rearrange("q (c r) t -> q c t r", r=4),
                in0=w_raw[k][:].rearrange("q (t c) -> q t c", t=PACK)[:, :, cols].rearrange("q t (c r) -> q c t r", r=4),
                scalar1=1.0, scalar2=0.0, op0=MULT, op1=ADD,
            )

        def quantise_weights(k):
            nc.vector.quantize_mx(
                out=w_codes[k][:].bitcast(FP8X4),
                scales=w_scales[k][:],
                in_=w_grouped[k][:].rearrange("q c t -> q (c t)"),
            )

        load_w_base(2)
        load_a(0, 0)
        load_w_lora(2)
        load_x(0, 0)
        load_a(1, 0)
        load_x(0, 1)
        load_x(0, 2)
        load_x(1, 0)
        load_a(0, 1)
        load_x(0, 3)
        load_w_lora(1)
        load_w_base(1)
        load_x(0, 4)
        load_w_lora(0)
        load_w_base(0)
        load_a(1, 1)
        load_x(1, 1)
        for pair in range(2, PAIRS):
            load_a(pair, 0)
            load_x(pair, 0)

        make_identity(nc, ident_bf16[:])
        make_identity(nc, ident_f32[:])

        a_t = {}
        x_codes = {}
        x_scales = {}
        x_words = {}
        stage_of = {}

        for step in range(-FIRST_LEAD, STEPS):
            x_step = step + X_LEAD
            lora_step = step + LORA_LEAD
            a_step = step + A_LEAD
            do_x = 0 <= x_step < STEPS
            do_lora = 0 <= lora_step < STEPS
            p_step = step + PERMUTE_LEAD
            do_p = PERMUTE_FROM <= p_step < STEPS
            do_a = 0 <= a_step < STEPS and a_step % GROUP == 0
            do_base = step >= 0

            if do_x:
                xt = xt_banks.tile([P, PAIR, HALVES, P], F32, name="xt")
                x_grouped = x_work.tile([P, PAIR * P * PACK], BF16, name="x_part", align_bytes=64)
                x_codes[x_step] = ready.tile([P, PAIR * P], U32, name="x_codes", align_bytes=64)
                x_scales[x_step] = ready.tile([P, PAIR * P], U8, name="x_scales", align_bytes=64)
            if do_p:
                x_words[p_step] = x_work.tile([P, P * PACK], BF16, name="x_part", align_bytes=64)
            if do_a:
                a_group = a_step // GROUP
                at = at_banks.tile([P, GROUP, PAIR, P], BF16, name="at")
                a_t[a_group] = a_ready.tile([P, GROUP, PAIR, P], BF16, name="a_t")
            lora = {}
            base = {}

            def transpose_x(i):
                pair, j = PLACES[x_step]
                x_tile, first = block_of(x_sb, pair, i, j, MUL)
                for u in range(HALVES):
                    if u == 1 and x_step in x_words:
                        words = x_words[x_step][:].bitcast(F32)[:, i * P : (i + 1) * P]
                    else:
                        words = x_tile[:].bitcast(F32)[:, first // 2 + u : first // 2 + HALVES * P : HALVES]
                    nc.tensor.transpose(xt[:, i, u, :], words, ident_f32[:])

            def permute_x():
                pair, j = PLACES[p_step]
                first, blocks, x_tile = piece_of(x_sb, pair, j)
                words = x_tile[:].rearrange("p (i b q u e) -> p i b q u e", i=PAIR, b=blocks, u=HALVES, e=2)
                nc.gpsimd.tensor_scalar(
                    out=x_words[p_step][:].rearrange("p (i q e) -> p i q e", i=PAIR, e=2),
                    in0=words[:, :, j - first, :, 1, :],
                    scalar1=1.0, scalar2=0.0, op0=MULT, op1=ADD,
                )

            def transpose_a():
                for later in range(GROUP):
                    pair, j = PLACES[a_step + later]
                    for i in range(PAIR):
                        a_tile, first = block_of(a_sb, pair, i, j, RANK)
                        nc.tensor.transpose(at[:, later, i, :], a_tile[:, first : first + RANK], ident_bf16[:])

            def multiply_lora(i):
                pair, j = PLACES[lora_step]
                lora[i] = lora_banks.tile([P, MUL], F32, name="lora_ps")
                nc.tensor.matmul(
                    lora[i][:],
                    lhsT=a_t[lora_step // GROUP][:, lora_step % GROUP, i, :],
                    rhs=wb_sb[IRREP_OF_BLOCK[j]][:],
                    start=True,
                    stop=True,
                )

            def multiply_base(i):
                pair, j = PLACES[step]
                k = IRREP_OF_BLOCK[j]
                nodes = slice(i * P, (i + 1) * P)
                base[i] = base_banks.tile([P, MUL], F32, name="base_ps")
                nc.tensor.matmul_mx(
                    out=base[i][:],
                    lhsT=x_codes[step][:, nodes].bitcast(FP8X4),
                    lhsT_scale=x_scales[step][:, nodes],
                    rhs=w_codes[k][:].bitcast(FP8X4),
                    rhs_scale=w_scales[k][:],
                    start=True,
                    stop=True,
                )

            def scale_lora(i):
                tile, cols, together = stage_of[lora_step]
                nc.scalar.mul(out=tile[:, i, cols], in_=lora[i][:], mul=LORA_FACTOR)

            def group_x():
                nc.scalar.copy(
                    out=x_grouped[:].bitcast(F32).rearrange("q (i n u) -> q i n u", i=PAIR, u=HALVES),
                    in_=xt[:].rearrange("q i u n -> q i n u"),
                )

            def quantise_x():
                nc.vector.quantize_mx(
                    out=x_codes[x_step][:].bitcast(FP8X4), scales=x_scales[x_step][:], in_=x_grouped[:]
                )

            def finish(i):
                tile, cols, together = stage_of[step]
                nc.vector.scalar_tensor_tensor(
                    out=tile[:, i, cols], in0=base[i][:], scalar=BASE_FACTOR, in1=tile[:, i, cols],
                    op0=MULT, op1=ADD,
                )

            if do_lora:
                pair, j = PLACES[lora_step]
                together = 1 if lora_step >= STEPS - GROUP else GROUP
                if j % together == together - 1:
                    stage = stages.tile([P, PAIR, together * MUL], F32, name="stage")
                stage_of[lora_step] = (stage, slice((j % together) * MUL, (j % together + 1) * MUL), together)

            for k in range(IRREPS):
                part = step + GROUP_WEIGHTS_LEAD - FIRST_USE[k]
                if FIRST_USE[k] > 0 and 0 <= part < WEIGHT_PARTS:
                    group_weights_part(k, part, x_codes[x_step - 1])
            if do_p:
                permute_x()
            if do_lora:
                multiply_lora(0)
            if do_x:
                transpose_x(0)
            if do_lora:
                multiply_lora(1)
            if do_x:
                transpose_x(1)
            if do_a:
                transpose_a()
            if do_base:
                multiply_base(0)
                multiply_base(1)
            if do_lora:
                scale_lora(0)
                scale_lora(1)
            if do_x:
                group_x()
            if do_a:
                nc.vector.tensor_copy(out=a_t[a_group][:], in_=at[:])
            if do_base:
                finish(0)
                finish(1)
            if do_x:
                quantise_x()
            if step == FIRST_USE[IRREP_OF_BLOCK[BLOCKS - 1]] - FIRST_LEAD:
                group_weights(IRREP_OF_BLOCK[BLOCKS - 1])
            for k in range(IRREPS):
                if step + WEIGHT_LEAD == FIRST_USE[k]:
                    quantise_weights(k)
            if do_base:
                pair, j = PLACES[step]
                tile, cols, together = stage_of[step]
                parts = PAIR if step == STEPS - 1 else 1
                if j % together == 0:
                    for part in range(parts):
                        rows = slice(part * PAIR // parts, (part + 1) * PAIR // parts)
                        nc.sync.dma_start(
                            out=out_rows[:, PAIR * pair + rows.start : PAIR * pair + rows.stop, j * MUL : (j + together) * MUL],
                            in_=tile[:, rows, :],
                        )
